import numpy as np
import ml_dtypes


def mxq(x, axis, fmt="e4m3"):
    dtype, down = {"e4m3": (ml_dtypes.float8_e4m3fn, 7), "e5m2": (ml_dtypes.float8_e5m2, 14)}[fmt]
    v = np.moveaxis(np.asarray(x, np.float32).astype(ml_dtypes.bfloat16).astype(np.float64), axis, -1)
    blocks = v.reshape(v.shape[:-1] + (-1, 32))
    amax = np.abs(blocks).max(-1, keepdims=True)
    byte = np.maximum(np.where(amax > 0, np.frexp(amax)[1] - 1 + 127, 0) - down, 1)
    scale = np.exp2(byte - 127.0)
    codes = (blocks / scale).astype(np.float32).astype(dtype).astype(np.float64)
    return np.moveaxis((codes * scale).reshape(v.shape), -1, axis)


WIDE = False


def mx_kscale(k):
    if not WIDE:
        return np.ones(k)
    levels = np.array([10, -10, 5, -5, 0])
    if k % 512:
        return np.exp2(np.random.permutation(np.resize(levels, k // 32))).repeat(32)
    a = np.empty((k // 512, 16))
    for p in range(k // 512):
        a[p, :8] = np.random.permutation(np.resize(levels, 8))
        for g in range(8):
            far = levels[np.abs(levels - a[p, g]) >= 10]
            a[p, g + 8] = far[np.random.randint(len(far))]
    return np.exp2(a.ravel()).repeat(32)


BF16 = ml_dtypes.bfloat16


def bf(x):
    return np.asarray(x, np.float32).astype(BF16)


def f64(x):
    return np.asarray(x).astype(np.float64)


B, H, L, D = 2, 2, 1024, 1024
NEG = -100.0


def setup_inputs():
    s = mx_kscale(D)
    return {"q": bf(np.random.standard_normal((B, H, L, D)) * s),
            "e": bf(np.random.standard_normal((H, L, D)) / np.sqrt(D) / s)}


def core(q, e):
    rel = mxq(f64(q), 3, "e4m3") @ mxq(f64(e), 2, "e4m3").transpose(0, 2, 1)
    rel = rel.reshape(B * H, L, L)
    rel = np.pad(rel, ((0, 0), (0, 0), (1, 0)), constant_values=NEG)
    rel = rel.reshape(B * H, L + 1, L)[:, 1:, :][:, :L, :]
    mask = np.triu(np.ones((L, L), dtype=bool), k=1)
    rel = np.where(mask[None, :, :], 0.0, rel)
    return rel.reshape(B, H, L, L)


def e4m3fn_bytes(y):
    return np.clip(np.asarray(y, np.float64), -448.0, 448.0).astype(np.float32).astype(ml_dtypes.float8_e4m3fn).view(np.uint8)


def reference(q, e):
    out = core(q, e)
    s = np.max(np.abs(out), axis=-1, keepdims=True) / 448.0
    return out, e4m3fn_bytes(out / s)

@@ -1,0 +1,291 @@
+from contextlib import ExitStack
+
+import concourse.mybir as mybir
+from concourse.masks import make_identity
+
+B, H, L, D = 2, 2, 1024, 1024
+FLOPS = B * H * L * (L + 1) * D
+
+F32 = mybir.dt.float32
+BF16 = mybir.dt.bfloat16
+U32 = mybir.dt.uint32
+U8 = mybir.dt.uint8
+FP8 = mybir.dt.float8_e4m3fn
+FP8X4 = mybir.dt.float8_e4m3fn_x4
+ALU = mybir.AluOpType
+ACT = mybir.ActivationFunctionType
+AX = mybir.AxisListType
+
+P = 128
+NT = L // P
+R = 2
+PAIRS = P // R
+RUN = L + 1
+BANK = 512
+BACK_AFTER = 2
+CAST_AFTER = (8, 6)
+
+
+def tile_subsampledrelativeattention_kernel(tc, q, e, out_0, out_1):
+    nc = tc.nc
+    mat0 = out_0.rearrange("b h i j -> b h (i j)")
+    mat1 = out_1.rearrange("b h i j -> b h (i j)")
+    steps = [(h, i) for h in range(H) for i in range(NT)]
+    n_steps = len(steps)
+
+    with ExitStack() as ctx:
+        keep = ctx.enter_context(tc.tile_pool(name="keep", bufs=1))
+        grp = ctx.enter_context(tc.tile_pool(name="grp", bufs=3))
+        qcp = ctx.enter_context(tc.tile_pool(name="qcp", bufs=3))
+        small = ctx.enter_context(tc.tile_pool(name="small", bufs=3))
+        back = ctx.enter_context(tc.tile_pool(name="back", bufs=2))
+        tp = ctx.enter_context(tc.psum_pool(name="tp", bufs=4))
+        mm = ctx.enter_context(tc.psum_pool(name="mm", bufs=4))
+
+        ident = keep.tile([P, P], F32, name="ident")
+        make_identity(nc, ident[:])
+        mask = keep.tile([P, R, P], F32, name="mask")
+        nc.gpsimd.memset(mask[:], 1.0)
+        for r in range(R):
+            for c0 in range(2):
+                nc.gpsimd.affine_select(
+                    out=mask[:, r, c0:P:2], in_=mask[:, r, c0:P:2], pattern=[[2, P // 2]], compare_op=ALU.is_ge,
+                    fill=0.0, base=r + c0 - (P - 1) - (1 - (c0 + r) % 2), channel_multiplier=1,
+                )
+        zcol = keep.tile([P, 1], F32, name="zcol")
+        nc.vector.memset(zcol[:], 0.0)
+
+        ctx.enter_context(tc.manual_schedule())
+
+        raw_q = []
+        raw_e = {}
+        for s in range(n_steps):
+            h, i = steps[s]
+            t = NT - 1 - i
+            if t % 2 == 1:
+                x = keep.tile([P, 2, D], BF16, name="re%d_%d" % (h, t // 2))
+                nc.sync.dma_start(out=x[:], in_=e[h, (t - 1) * P:(t + 1) * P, :].rearrange("(t p) k -> p t k", p=P))
+                raw_e[(h, t // 2)] = x
+            x = keep.tile([P, R, D], BF16, name="rq%d" % s)
+            nc.sync.dma_start(
+                out=x[:].rearrange("p r k -> p (r k)"),
+                in_=q[:, h, i * P:(i + 1) * P, :].rearrange("b (a r) k -> a b (r k)", r=R),
+            )
+            raw_q.append(x)
+
+        ec = []
+        es = []
+        for h in range(H):
+            x = keep.tile([P, 2, L], U32, name="ec%d" % h, align_bytes=64)
+            ec.append(x)
+            x = keep.tile([P, 2, L], U8, name="es%d" % h, align_bytes=64)
+            es.append(x)
+
+        res = []
+        o8 = []
+        for i in range(NT):
+            x = keep.tile([P, R * RUN], F32, name="res%d" % i)
+            res.append(x)
+            x = keep.tile([P, R * (RUN if i > 0 else L)], FP8, name="o8_%d" % i)
+            o8.append(x)
+        fac = []
+        for s in range(n_steps):
+            x = keep.tile([P, R], F32, name="fac%d" % s)
+            fac.append(x)
+
+        def plain_cast(r, out, in_):
+            if r == 0:
+                nc.vector.tensor_copy(out=out, in_=in_, saturate=False)
+            else:
+                nc.scalar.copy(out=out, in_=in_, saturate=False)
+
+        def scaled_cast(r, out, in_, f):
+            if r == 0:
+                nc.vector.tensor_scalar(out=out, in0=in_, scalar1=f, scalar2=None, op0=ALU.mult, saturate=False)
+            else:
+                nc.scalar.activation(out=out, in_=in_, func=ACT.Identity, scale=f, bias=zcol[:, 0:1], saturate=False)
+
+        def transposes(s):
+            h, i = steps[s]
+            t = NT - 1 - i
+            items = [("e", t, raw_e[(h, t // 2)][:, t % 2, :])]
+            items.extend([("q", r, raw_q[s][:, r, :]) for r in range(R)])
+            made = []
+            for kind, idx, src in items:
+                words = src.bitcast(F32)
+                xt = tp.tile([P, 2, 2, P], F32, name="xt", tag="xt")
+                for g in range(2):
+                    for u in range(2):
+                        nc.tensor.transpose(xt[:, g, u, :], words[:, 256 * g + u:256 * (g + 1):2], ident[:])
+                made.append((kind, idx, xt))
+            return made
+
+        def copies(made):
+            grouped = []
+            gq = grp.tile([P, R, 2, P, 4], BF16, name="gq", tag="gq", align_bytes=64)
+            for kind, idx, xt in made:
+                if kind == "q":
+                    nc.scalar.copy(out=gq[:, idx].bitcast(F32), in_=xt[:].rearrange("p g u r -> p g r u"))
+                else:
+                    ge = grp.tile([P, 2, P, 4], BF16, name="ge", tag="ge", align_bytes=64)
+                    nc.scalar.copy(out=ge[:].bitcast(F32), in_=xt[:].rearrange("p g u r -> p g r u"))
+                    grouped.append((idx, ge))
+            return grouped, gq
+
+        def quantize(s, both):
+            h, i = steps[s]
+            grouped, gq = both
+            for idx, ge in grouped:
+                cols = slice(idx * P, (idx + 1) * P)
+                for g in range(2):
+                    nc.vector.quantize_mx(
+                        out=ec[h][:, g, cols].bitcast(FP8X4), scales=es[h][:, g, cols],
+                        in_=ge[:, g, :, :].rearrange("p r t -> p (r t)"),
+                    )
+            qc = qcp.tile([P, R * 2 * P], U32, name="qc", tag="qc", align_bytes=64)
+            qs = qcp.tile([P, R * 2 * P], U8, name="qs", tag="qs", align_bytes=64)
+            nc.vector.quantize_mx(
+                out=qc[:].bitcast(FP8X4), scales=qs[:], in_=gq[:].rearrange("p b g r t -> p (b g r t)"),
+            )
+            return qc, qs
+
+        def multiply(s, codes):
+            h, i = steps[s]
+            width = (i + 1) * P
+            m0 = L - width
+            qc, qs = codes
+            banks = []
+            for r in range(R):
+                for c0 in range(0, width, BANK):
+                    bw = min(BANK, width - c0)
+                    acc = mm.tile([P, BANK], F32, name="acc", tag="acc")
+                    groups = [(0, 256), (256, 128)] if bw == 384 else [(0, bw)]
+                    for g0, n in groups:
+                        cols = slice(m0 + c0 + g0, m0 + c0 + g0 + n)
+                        for g in range(2):
+                            w = slice((r * 2 + g) * P, (r * 2 + g + 1) * P)
+                            nc.tensor.matmul_mx(
+                                out=acc[:, g0:g0 + n],
+                                lhsT=qc[:, w].bitcast(FP8X4), lhsT_scale=qs[:, w],
+                                rhs=ec[h][:, g, cols].bitcast(FP8X4), rhs_scale=es[h][:, g, cols],
+                                start=(g == 0), stop=(g == 1),
+                            )
+                    banks.append((r, c0, bw, acc))
+            return banks
+
+        def empty_diag(s, banks):
+            h, i = steps[s]
+            z = RUN - (i + 1) * P
+            for r, c0, bw, acc in banks:
+                if c0 == 0:
+                    d0 = r * RUN + z
+                    nc.vector.tensor_tensor(out=res[i][:, d0:d0 + P], in0=acc[:, 0:P], in1=mask[:, r, :], op=ALU.mult)
+
+        def skewed(mat, h, i):
+            lo = i * P * RUN - L
+            return mat[:, h, lo:lo + P * RUN].rearrange("b (a y) -> a b y", y=R * RUN)
+
+        def empty_rest(s, banks):
+            h, i = steps[s]
+            z = RUN - (i + 1) * P
+            for r, c0, bw, acc in banks:
+                lo = P if c0 == 0 else 0
+                d0 = r * RUN + z + c0
+                if bw > lo:
+                    nc.scalar.copy(out=res[i][:, d0 + lo:d0 + bw], in_=acc[:, lo:bw])
+            for b in range(B):
+                if i > 0:
+                    lo = i * P * RUN - L
+                    nc.sync.dma_start(
+                        out=mat0[b, h, lo:lo + P * RUN].rearrange("(a y) -> a y", y=R * RUN), in_=res[i][b:P:B, :],
+                    )
+                else:
+                    nc.sync.dma_start(
+                        out=mat0[b, h, 0:P * RUN].rearrange("(a y) -> a y", y=R * RUN)[:, 0:RUN + 1],
+                        in_=res[0][b:P:B, L:R * RUN],
+                    )
+                    nc.gpsimd.dma_start(
+                        out=mat0[b, h, RUN + 1:RUN + 1 + (PAIRS - 1) * R * RUN].rearrange(
+                            "(a y) -> a y", y=R * RUN)[:, 0:L],
+                        in_=res[0][B + b:P:B, 0:L],
+                    )
+
+        def row_factors(s):
+            h, i = steps[s]
+            width = (i + 1) * P
+            z = RUN - width
+            am = small.tile([P, R], F32, name="am", tag="am")
+            for r in range(R):
+                nc.vector.tensor_reduce(
+                    out=am[:, r:r + 1], in_=res[i][:, r * RUN + z:(r + 1) * RUN], axis=AX.X, op=ALU.max,
+                    apply_absolute_value=True,
+                )
+            rc = small.tile([P, R], F32, name="rc", tag="rc")
+            nc.vector.reciprocal(out=rc[:], in_=am[:])
+            nc.gpsimd.tensor_scalar(out=fac[s][:], in0=rc[:], scalar1=448.0, scalar2=0.0, op0=ALU.mult, op1=ALU.add)
+
+        def finish(s):
+            h, i = steps[s]
+            z = RUN - (i + 1) * P
+            f0 = fac[s][:, 0:1]
+            f1 = fac[s][:, 1:2]
+            edge = RUN + 3
+            if z == 1:
+                scaled_cast(0, o8[i][:, 0:RUN], res[i][:, 0:RUN], f0)
+                scaled_cast(0, o8[i][:, RUN:edge], res[i][:, RUN:edge], f1)
+                scaled_cast(1, o8[i][:, edge:R * RUN], res[i][:, edge:R * RUN], f1)
+            elif h == 0:
+                scaled_cast(0, o8[i][:, 0:edge], res[i][:, 0:edge], f0)
+                scaled_cast(1, o8[i][:, edge:R * RUN], res[i][:, edge:R * RUN], f1)
+            else:
+                scaled_cast(0, o8[i][:, z:RUN], res[i][:, z:RUN], f0)
+                scaled_cast(1, o8[i][:, RUN + z:R * RUN], res[i][:, RUN + z:R * RUN], f1)
+            nc.sync.dma_start(out=skewed(mat1, h, i), in_=o8[i][:].bitcast(U8))
+
+        def load_back(s):
+            h, i = steps[s]
+            lb = back.tile([P, R, P], F32, name="lb", tag="lb")
+            for b in range(B):
+                nc.sync.dma_start(out=lb[b:P:B, :, :], in_=out_0[b, h, 0:P, 0:P].rearrange("(a r) j -> a r j", r=R))
+            return lb
+
+        def finish_first(s, lb):
+            h, i = steps[s]
+            for r in range(R):
+                if h == 0:
+                    plain_cast(r, o8[0][:, r * L + P:(r + 1) * L], res[0][:, 0:L - P])
+                scaled_cast(r, o8[0][:, r * L:r * L + P], lb[:, r, :], fac[s][:, r:r + 1])
+            nc.sync.dma_start(
+                out=out_1[:, h, 0:P, :].rearrange("b (a r) j -> a b (r j)", r=R), in_=o8[0][:].bitcast(U8),
+            )
+
+        for i in range(NT):
+            nc.vector.memset(res[i][:].rearrange("p (r y) -> p r y", r=R)[:, :, 0:RUN - (i + 1) * P], 0.0)
+
+        codes = {0: quantize(0, copies(transposes(0)))}
+        loaded = {}
+        for s in range(n_steps + 1):
+            nxt = s + 1
+            made = None
+            banks = None
+            if nxt < n_steps:
+                made = transposes(nxt)
+            if s < n_steps:
+                banks = multiply(s, codes[s])
+                empty_diag(s, banks)
+            both = None
+            if nxt < n_steps:
+                both = copies(made)
+            if s < n_steps:
+                empty_rest(s, banks)
+            if nxt < n_steps:
+                codes[nxt] = quantize(nxt, both)
+            if s >= 1 and steps[s - 1][1] > 0:
+                finish(s - 1)
+            for h in range(H):
+                if s == h * NT + BACK_AFTER:
+                    loaded[h] = load_back(h * NT)
+                if s == h * NT + CAST_AFTER[h]:
+                    finish_first(h * NT, loaded[h])
+            if s < n_steps:
+                row_factors(s)

@@ -8,6 +8,7 @@ FLOPS = B * H * L * (L + 1) * D
 
 F32 = mybir.dt.float32
 BF16 = mybir.dt.bfloat16
+I32 = mybir.dt.int32
 U32 = mybir.dt.uint32
 U8 = mybir.dt.uint8
 FP8 = mybir.dt.float8_e4m3fn
@@ -18,25 +19,48 @@ AX = mybir.AxisListType
 
 P = 128
 NT = L // P
-R = 2
-PAIRS = P // R
+SLOTS = P // B
 RUN = L + 1
 BANK = 512
-BACK_AFTER = 2
-CAST_AFTER = (8, 6)
+GROUPS = ((0, 2), (128, 2), (256, 3), (448, 3), (640, 3), (832, 3))
+ORDER = ((0, 1, 2, 3, 4, 5), (0, 5, 4, 3, 2, 1))
+OWN_TILES = (5,)
+AHEAD = 2
+CAST_LAG = 1
+BACK_AFTER = 4
+CAST_AFTER = (16, 12)
 
 
 def tile_subsampledrelativeattention_kernel(tc, q, e, out_0, out_1):
     nc = tc.nc
     mat0 = out_0.rearrange("b h i j -> b h (i j)")
     mat1 = out_1.rearrange("b h i j -> b h (i j)")
-    steps = [(h, i) for h in range(H) for i in range(NT)]
-    n_steps = len(steps)
+    n_groups = len(GROUPS)
+    units = [(h, j, r) for h in range(H) for j in ORDER[h] for r in range(GROUPS[j][1])]
+    n_units = len(units)
+    need = [row0 + SLOTS * rows for row0, rows in GROUPS]
+    wide = [-(-n // P) * P for n in need]
+
+    wanted = []
+    have = [NT] * H
+    for k in range(n_units):
+        h, j, r = units[k]
+        for t in range(have[h] - 1, (L - wide[j]) // P - 1, -1):
+            wanted.append((k - AHEAD, h, t))
+        have[h] = min(have[h], (L - wide[j]) // P)
+    plan = [[] for n in range(n_units)]
+    at = n_units
+    for due, h, t in reversed(wanted):
+        at = max(min(due, at - 1), -AHEAD)
+        plan[AHEAD + at].insert(0, ("e", h, t))
+    for k in range(n_units):
+        plan[k].append(("q", k, 0))
+    jobs = [job for part in plan for job in part]
 
     with ExitStack() as ctx:
         keep = ctx.enter_context(tc.tile_pool(name="keep", bufs=1))
-        grp = ctx.enter_context(tc.tile_pool(name="grp", bufs=3))
-        qcp = ctx.enter_context(tc.tile_pool(name="qcp", bufs=3))
+        grp = ctx.enter_context(tc.tile_pool(name="grp", bufs=4))
+        qcp = ctx.enter_context(tc.tile_pool(name="qcp", bufs=4))
         small = ctx.enter_context(tc.tile_pool(name="small", bufs=3))
         back = ctx.enter_context(tc.tile_pool(name="back", bufs=2))
         tp = ctx.enter_context(tc.psum_pool(name="tp", bufs=4))
@@ -44,34 +68,54 @@ def tile_subsampledrelativeattention_kernel(tc, q, e, out_0, out_1):
 
         ident = keep.tile([P, P], F32, name="ident")
         make_identity(nc, ident[:])
-        mask = keep.tile([P, R, P], F32, name="mask")
-        nc.gpsimd.memset(mask[:], 1.0)
-        for r in range(R):
-            for c0 in range(2):
-                nc.gpsimd.affine_select(
-                    out=mask[:, r, c0:P:2], in_=mask[:, r, c0:P:2], pattern=[[2, P // 2]], compare_op=ALU.is_ge,
-                    fill=0.0, base=r + c0 - (P - 1) - (1 - (c0 + r) % 2), channel_multiplier=1,
-                )
         zcol = keep.tile([P, 1], F32, name="zcol")
         nc.vector.memset(zcol[:], 0.0)
 
+        part_i = keep.tile([P, 1], I32, name="part_i")
+        nc.gpsimd.iota(part_i[:], pattern=[[0, 1]], base=0, channel_multiplier=1)
+        col_i = keep.tile([P, SLOTS * 3], I32, name="col_i")
+        nc.gpsimd.iota(col_i[:], pattern=[[1, SLOTS * 3]], base=0, channel_multiplier=0)
+        slot_i = keep.tile([P, 1], I32, name="slot_i")
+        nc.vector.tensor_scalar(out=slot_i[:], in0=part_i[:], scalar1=1, scalar2=None, op0=ALU.arith_shift_right)
+        slot_f = keep.tile([P, 1], F32, name="slot_f")
+        nc.vector.tensor_copy(out=slot_f[:], in_=slot_i[:])
+        col_f = keep.tile([P, SLOTS * 3], F32, name="col_f")
+        nc.vector.tensor_copy(out=col_f[:], in_=col_i[:])
+        mask = {}
+        for rows in (2, 3):
+            first = keep.tile([P, rows], F32, name="first%d" % rows)
+            x = keep.tile([P, rows, SLOTS * rows], F32, name="mask%d" % rows)
+            for r in range(rows):
+                nc.vector.tensor_scalar(
+                    out=first[:, r:r + 1], in0=slot_f[:], scalar1=-1.0 * rows, scalar2=1.0 * (SLOTS * rows - 1 - r),
+                    op0=ALU.mult, op1=ALU.add,
+                )
+                nc.vector.tensor_scalar(
+                    out=x[:, r, :], in0=col_f[:, 0:SLOTS * rows], scalar1=first[:, r:r + 1], scalar2=None,
+                    op0=ALU.is_ge,
+                )
+            mask[rows] = x
+
         ctx.enter_context(tc.manual_schedule())
 
-        raw_q = []
+        raw_q = {}
         raw_e = {}
-        for s in range(n_steps):
-            h, i = steps[s]
-            t = NT - 1 - i
-            if t % 2 == 1:
-                x = keep.tile([P, 2, D], BF16, name="re%d_%d" % (h, t // 2))
-                nc.sync.dma_start(out=x[:], in_=e[h, (t - 1) * P:(t + 1) * P, :].rearrange("(t p) k -> p t k", p=P))
-                raw_e[(h, t // 2)] = x
-            x = keep.tile([P, R, D], BF16, name="rq%d" % s)
-            nc.sync.dma_start(
-                out=x[:].rearrange("p r k -> p (r k)"),
-                in_=q[:, h, i * P:(i + 1) * P, :].rearrange("b (a r) k -> a b (r k)", r=R),
-            )
-            raw_q.append(x)
+        for kind, a0, a1 in jobs:
+            if kind == "e" and a1 % 2 == 1:
+                x = keep.tile([P, 2, D], BF16, name="re%d_%d" % (a0, a1 // 2))
+                nc.sync.dma_start(
+                    out=x[:], in_=e[a0, (a1 - 1) * P:(a1 + 1) * P, :].rearrange("(t p) k -> p t k", p=P),
+                )
+                raw_e[(a0, a1 // 2)] = x
+            if kind == "q" and units[a0][2] == 0:
+                h, j, r = units[a0]
+                row0, rows = GROUPS[j]
+                x = keep.tile([P, rows, D], BF16, name="rq%d_%d" % (h, j))
+                nc.sync.dma_start(
+                    out=x[:].rearrange("p r k -> p (r k)"),
+                    in_=q[:, h, row0:row0 + SLOTS * rows, :].rearrange("b (a r) k -> a b (r k)", r=rows),
+                )
+                raw_q[(h, j)] = x
 
         ec = []
         es = []
@@ -81,211 +125,255 @@ def tile_subsampledrelativeattention_kernel(tc, q, e, out_0, out_1):
             x = keep.tile([P, 2, L], U8, name="es%d" % h, align_bytes=64)
             es.append(x)
 
-        res = []
-        o8 = []
-        for i in range(NT):
-            x = keep.tile([P, R * RUN], F32, name="res%d" % i)
-            res.append(x)
-            x = keep.tile([P, R * (RUN if i > 0 else L)], FP8, name="o8_%d" % i)
-            o8.append(x)
-        fac = []
-        for s in range(n_steps):
-            x = keep.tile([P, R], F32, name="fac%d" % s)
-            fac.append(x)
-
-        def plain_cast(r, out, in_):
-            if r == 0:
-                nc.vector.tensor_copy(out=out, in_=in_, saturate=False)
-            else:
-                nc.scalar.copy(out=out, in_=in_, saturate=False)
-
-        def scaled_cast(r, out, in_, f):
-            if r == 0:
-                nc.vector.tensor_scalar(out=out, in0=in_, scalar1=f, scalar2=None, op0=ALU.mult, saturate=False)
-            else:
-                nc.scalar.activation(out=out, in_=in_, func=ACT.Identity, scale=f, bias=zcol[:, 0:1], saturate=False)
-
-        def transposes(s):
-            h, i = steps[s]
-            t = NT - 1 - i
-            items = [("e", t, raw_e[(h, t // 2)][:, t % 2, :])]
-            items.extend([("q", r, raw_q[s][:, r, :]) for r in range(R)])
-            made = []
-            for kind, idx, src in items:
-                words = src.bitcast(F32)
-                xt = tp.tile([P, 2, 2, P], F32, name="xt", tag="xt")
-                for g in range(2):
-                    for u in range(2):
-                        nc.tensor.transpose(xt[:, g, u, :], words[:, 256 * g + u:256 * (g + 1):2], ident[:])
-                made.append((kind, idx, xt))
-            return made
-
-        def copies(made):
-            grouped = []
-            gq = grp.tile([P, R, 2, P, 4], BF16, name="gq", tag="gq", align_bytes=64)
-            for kind, idx, xt in made:
-                if kind == "q":
-                    nc.scalar.copy(out=gq[:, idx].bitcast(F32), in_=xt[:].rearrange("p g u r -> p g r u"))
+        res_of = {}
+        o8_of = {}
+        for h in range(H):
+            for j in range(n_groups):
+                rows = GROUPS[j][1]
+                if h == 0 or j in OWN_TILES:
+                    x = keep.tile([P, rows * RUN], F32, name="res%d_%d" % (h, j))
+                    res_of[(h, j)] = x
+                    x = keep.tile([P, rows * (RUN if j > 0 else L)], FP8, name="o8_%d_%d" % (h, j))
+                    o8_of[(h, j)] = x
                 else:
-                    ge = grp.tile([P, 2, P, 4], BF16, name="ge", tag="ge", align_bytes=64)
-                    nc.scalar.copy(out=ge[:].bitcast(F32), in_=xt[:].rearrange("p g u r -> p g r u"))
-                    grouped.append((idx, ge))
-            return grouped, gq
+                    res_of[(h, j)] = res_of[(0, j)]
+                    o8_of[(h, j)] = o8_of[(0, j)]
+        fac = {}
+        for h in range(H):
+            for j in range(n_groups):
+                x = keep.tile([P, GROUPS[j][1]], F32, name="fac%d_%d" % (h, j))
+                fac[(h, j)] = x
 
-        def quantize(s, both):
-            h, i = steps[s]
-            grouped, gq = both
-            for idx, ge in grouped:
-                cols = slice(idx * P, (idx + 1) * P)
+        def plain_cast(on_scalar, out, in_):
+            if on_scalar:
+                nc.scalar.copy(out=out, in_=in_, saturate=False)
+            else:
+                nc.vector.tensor_copy(out=out, in_=in_, saturate=False)
+
+        def scaled_cast(on_scalar, out, in_, f):
+            if on_scalar:
+                nc.scalar.activation(out=out, in_=in_, func=ACT.Identity, scale=f, bias=zcol[:, 0:1], saturate=False)
+            else:
+                nc.vector.tensor_scalar(out=out, in0=in_, scalar1=f, scalar2=None, op0=ALU.mult, saturate=False)
+
+        def transposes(job):
+            kind, a0, a1 = job
+            if kind == "e":
+                src = raw_e[(a0, a1 // 2)][:, a1 % 2, :]
+            else:
+                h, j, r = units[a0]
+                src = raw_q[(h, j)][:, r, :]
+            words = src.bitcast(F32)
+            xt = tp.tile([P, 2, 2, P], F32, name="xt", tag="xt")
+            for g in range(2):
+                for u in range(2):
+                    nc.tensor.transpose(xt[:, g, u, :], words[:, 256 * g + u:256 * (g + 1):2], ident[:])
+            return xt
+
+        def copy_out(xt):
+            gx = grp.tile([P, 2, P, 4], BF16, name="gx", tag="gx", align_bytes=64)
+            nc.scalar.copy(out=gx[:].bitcast(F32), in_=xt[:].rearrange("p g u r -> p g r u"))
+            return gx
+
+        codes = {}
+
+        def quantize(job, gx):
+            kind, a0, a1 = job
+            if kind == "e":
+                cols = slice(a1 * P, (a1 + 1) * P)
                 for g in range(2):
                     nc.vector.quantize_mx(
-                        out=ec[h][:, g, cols].bitcast(FP8X4), scales=es[h][:, g, cols],
-                        in_=ge[:, g, :, :].rearrange("p r t -> p (r t)"),
+                        out=ec[a0][:, g, cols].bitcast(FP8X4), scales=es[a0][:, g, cols],
+                        in_=gx[:, g, :, :].rearrange("p r t -> p (r t)"),
                     )
-            qc = qcp.tile([P, R * 2 * P], U32, name="qc", tag="qc", align_bytes=64)
-            qs = qcp.tile([P, R * 2 * P], U8, name="qs", tag="qs", align_bytes=64)
-            nc.vector.quantize_mx(
-                out=qc[:].bitcast(FP8X4), scales=qs[:], in_=gq[:].rearrange("p b g r t -> p (b g r t)"),
-            )
-            return qc, qs
+            else:
+                qc = qcp.tile([P, 2 * P], U32, name="qc", tag="qc", align_bytes=64)
+                qs = qcp.tile([P, 2 * P], U8, name="qs", tag="qs", align_bytes=64)
+                nc.vector.quantize_mx(
+                    out=qc[:].bitcast(FP8X4), scales=qs[:], in_=gx[:].rearrange("p g r t -> p (g r t)"),
+                )
+                codes[a0] = (qc, qs)
 
-        def multiply(s, codes):
-            h, i = steps[s]
-            width = (i + 1) * P
-            m0 = L - width
-            qc, qs = codes
+        def multiply(k):
+            h, j, r = units[k]
+            m0 = L - wide[j]
+            qc, qs = codes[k]
             banks = []
-            for r in range(R):
-                for c0 in range(0, width, BANK):
-                    bw = min(BANK, width - c0)
-                    acc = mm.tile([P, BANK], F32, name="acc", tag="acc")
-                    groups = [(0, 256), (256, 128)] if bw == 384 else [(0, bw)]
-                    for g0, n in groups:
-                        cols = slice(m0 + c0 + g0, m0 + c0 + g0 + n)
-                        for g in range(2):
-                            w = slice((r * 2 + g) * P, (r * 2 + g + 1) * P)
-                            nc.tensor.matmul_mx(
-                                out=acc[:, g0:g0 + n],
-                                lhsT=qc[:, w].bitcast(FP8X4), lhsT_scale=qs[:, w],
-                                rhs=ec[h][:, g, cols].bitcast(FP8X4), rhs_scale=es[h][:, g, cols],
-                                start=(g == 0), stop=(g == 1),
-                            )
-                    banks.append((r, c0, bw, acc))
+            for c0 in range(0, wide[j], BANK):
+                bw = min(BANK, wide[j] - c0)
+                acc = mm.tile([P, BANK], F32, name="acc", tag="acc")
+                pieces = [(0, 256), (256, 128)] if bw == 384 else [(0, bw)]
+                for g0, n in pieces:
+                    cols = slice(m0 + c0 + g0, m0 + c0 + g0 + n)
+                    for g in range(2):
+                        w = slice(g * P, (g + 1) * P)
+                        nc.tensor.matmul_mx(
+                            out=acc[:, g0:g0 + n],
+                            lhsT=qc[:, w].bitcast(FP8X4), lhsT_scale=qs[:, w],
+                            rhs=ec[h][:, g, cols].bitcast(FP8X4), rhs_scale=es[h][:, g, cols],
+                            start=(g == 0), stop=(g == 1),
+                        )
+                banks.append((c0, bw, acc))
             return banks
 
-        def empty_diag(s, banks):
-            h, i = steps[s]
-            z = RUN - (i + 1) * P
-            for r, c0, bw, acc in banks:
-                if c0 == 0:
-                    d0 = r * RUN + z
-                    nc.vector.tensor_tensor(out=res[i][:, d0:d0 + P], in0=acc[:, 0:P], in1=mask[:, r, :], op=ALU.mult)
+        def empty_diag(k, banks):
+            h, j, r = units[k]
+            rows = GROUPS[j][1]
+            skip = wide[j] - need[j]
+            d0 = r * RUN + RUN - wide[j] + skip
+            c0, bw, acc = banks[0]
+            nc.vector.tensor_tensor(
+                out=res_of[(h, j)][:, d0:d0 + SLOTS * rows], in0=acc[:, skip:skip + SLOTS * rows], in1=mask[rows][:, r, :],
+                op=ALU.mult,
+            )
 
-        def skewed(mat, h, i):
-            lo = i * P * RUN - L
-            return mat[:, h, lo:lo + P * RUN].rearrange("b (a y) -> a b y", y=R * RUN)
-
-        def empty_rest(s, banks):
-            h, i = steps[s]
-            z = RUN - (i + 1) * P
-            for r, c0, bw, acc in banks:
-                lo = P if c0 == 0 else 0
-                d0 = r * RUN + z + c0
+        def empty_rest(k, banks):
+            h, j, r = units[k]
+            rows = GROUPS[j][1]
+            skip = wide[j] - need[j]
+            for c0, bw, acc in banks:
+                lo = skip + SLOTS * rows if c0 == 0 else 0
+                d0 = r * RUN + RUN - wide[j] + c0
                 if bw > lo:
-                    nc.scalar.copy(out=res[i][:, d0 + lo:d0 + bw], in_=acc[:, lo:bw])
+                    nc.scalar.copy(out=res_of[(h, j)][:, d0 + lo:d0 + bw], in_=acc[:, lo:bw])
+
+        def store_rows(h, j):
+            row0, rows = GROUPS[j]
             for b in range(B):
-                if i > 0:
-                    lo = i * P * RUN - L
+                if j > 0:
+                    lo = row0 * RUN - L
                     nc.sync.dma_start(
-                        out=mat0[b, h, lo:lo + P * RUN].rearrange("(a y) -> a y", y=R * RUN), in_=res[i][b:P:B, :],
+                        out=mat0[b, h, lo:lo + SLOTS * rows * RUN].rearrange("(a y) -> a y", y=rows * RUN),
+                        in_=res_of[(h, j)][b:P:B, :],
                     )
                 else:
                     nc.sync.dma_start(
-                        out=mat0[b, h, 0:P * RUN].rearrange("(a y) -> a y", y=R * RUN)[:, 0:RUN + 1],
-                        in_=res[0][b:P:B, L:R * RUN],
+                        out=mat0[b, h, 0:SLOTS * rows * RUN].rearrange("(a y) -> a y", y=rows * RUN)[:, 0:RUN + 1],
+                        in_=res_of[(h, 0)][b:P:B, L:rows * RUN],
                     )
                     nc.gpsimd.dma_start(
-                        out=mat0[b, h, RUN + 1:RUN + 1 + (PAIRS - 1) * R * RUN].rearrange(
-                            "(a y) -> a y", y=R * RUN)[:, 0:L],
-                        in_=res[0][B + b:P:B, 0:L],
+                        out=mat0[b, h, RUN + 1:RUN + 1 + (SLOTS - 1) * rows * RUN].rearrange(
+                            "(a y) -> a y", y=rows * RUN)[:, 0:L],
+                        in_=res_of[(h, 0)][B + b:P:B, 0:L],
                     )
 
-        def row_factors(s):
-            h, i = steps[s]
-            width = (i + 1) * P
-            z = RUN - width
-            am = small.tile([P, R], F32, name="am", tag="am")
-            for r in range(R):
-                nc.vector.tensor_reduce(
-                    out=am[:, r:r + 1], in_=res[i][:, r * RUN + z:(r + 1) * RUN], axis=AX.X, op=ALU.max,
-                    apply_absolute_value=True,
+        maxima = {}
+
+        def row_maximum(k):
+            h, j, r = units[k]
+            rows = GROUPS[j][1]
+            if r == 0:
+                am = small.tile([P, rows], F32, name="am", tag="am")
+                maxima[(h, j)] = am
+            am = maxima[(h, j)]
+            nc.vector.tensor_reduce(
+                out=am[:, r:r + 1], in_=res_of[(h, j)][:, r * RUN + RUN - need[j]:(r + 1) * RUN], axis=AX.X, op=ALU.max,
+                apply_absolute_value=True,
+            )
+            if r == rows - 1:
+                rc = small.tile([P, rows], F32, name="rc", tag="rc")
+                nc.vector.reciprocal(out=rc[:], in_=am[:])
+                nc.gpsimd.tensor_scalar(
+                    out=fac[(h, j)][:], in0=rc[:], scalar1=448.0, scalar2=0.0, op0=ALU.mult, op1=ALU.add,
                 )
-            rc = small.tile([P, R], F32, name="rc", tag="rc")
-            nc.vector.reciprocal(out=rc[:], in_=am[:])
-            nc.gpsimd.tensor_scalar(out=fac[s][:], in0=rc[:], scalar1=448.0, scalar2=0.0, op0=ALU.mult, op1=ALU.add)
 
-        def finish(s):
-            h, i = steps[s]
-            z = RUN - (i + 1) * P
-            f0 = fac[s][:, 0:1]
-            f1 = fac[s][:, 1:2]
-            edge = RUN + 3
-            if z == 1:
-                scaled_cast(0, o8[i][:, 0:RUN], res[i][:, 0:RUN], f0)
-                scaled_cast(0, o8[i][:, RUN:edge], res[i][:, RUN:edge], f1)
-                scaled_cast(1, o8[i][:, edge:R * RUN], res[i][:, edge:R * RUN], f1)
-            elif h == 0:
-                scaled_cast(0, o8[i][:, 0:edge], res[i][:, 0:edge], f0)
-                scaled_cast(1, o8[i][:, edge:R * RUN], res[i][:, edge:R * RUN], f1)
+        def finish(h, j):
+            row0, rows = GROUPS[j]
+            z = RUN - need[j]
+            f = fac[(h, j)]
+            new = h == 0 or j in OWN_TILES
+            last = (rows - 1) * RUN
+            if h == 0 or rows == 2:
+                cut = -(-last // 4) * 4 if z == 1 else (last + z) // 4 * 4
             else:
-                scaled_cast(0, o8[i][:, z:RUN], res[i][:, z:RUN], f0)
-                scaled_cast(1, o8[i][:, RUN + z:R * RUN], res[i][:, RUN + z:R * RUN], f1)
-            nc.sync.dma_start(out=skewed(mat1, h, i), in_=o8[i][:].bitcast(U8))
-
-        def load_back(s):
-            h, i = steps[s]
-            lb = back.tile([P, R, P], F32, name="lb", tag="lb")
-            for b in range(B):
-                nc.sync.dma_start(out=lb[b:P:B, :, :], in_=out_0[b, h, 0:P, 0:P].rearrange("(a r) j -> a r j", r=R))
-            return lb
-
-        def finish_first(s, lb):
-            h, i = steps[s]
-            for r in range(R):
-                if h == 0:
-                    plain_cast(r, o8[0][:, r * L + P:(r + 1) * L], res[0][:, 0:L - P])
-                scaled_cast(r, o8[0][:, r * L:r * L + P], lb[:, r, :], fac[s][:, r:r + 1])
+                cut = (last - need[j] // 2) // 4 * 4
+            for r in range(rows):
+                lo = r * RUN + (0 if new else z)
+                hi = (r + 1) * RUN
+                if h == 0 and z > 1 and r == rows - 1:
+                    lo = cut
+                if h == 0 and z > 1 and r == rows - 2:
+                    hi = -(-last // 4) * 4
+                if lo < cut:
+                    scaled_cast(
+                        False, o8_of[(h, j)][:, lo:min(hi, cut)], res_of[(h, j)][:, lo:min(hi, cut)], f[:, r:r + 1],
+                    )
+                if hi > cut:
+                    scaled_cast(
+                        True, o8_of[(h, j)][:, max(lo, cut):hi], res_of[(h, j)][:, max(lo, cut):hi], f[:, r:r + 1],
+                    )
+            lo = row0 * RUN - L
             nc.sync.dma_start(
-                out=out_1[:, h, 0:P, :].rearrange("b (a r) j -> a b (r j)", r=R), in_=o8[0][:].bitcast(U8),
+                out=mat1[:, h, lo:lo + SLOTS * rows * RUN].rearrange("b (a y) -> a b y", y=rows * RUN),
+                in_=o8_of[(h, j)][:].bitcast(U8),
             )
 
-        for i in range(NT):
-            nc.vector.memset(res[i][:].rearrange("p (r y) -> p r y", r=R)[:, :, 0:RUN - (i + 1) * P], 0.0)
+        def load_back(h):
+            rows = GROUPS[0][1]
+            lb = back.tile([P, rows, P], F32, name="lb", tag="lb")
+            for b in range(B):
+                nc.sync.dma_start(
+                    out=lb[b:P:B, :, :], in_=out_0[b, h, 0:P, 0:P].rearrange("(a r) j -> a r j", r=rows),
+                )
+            return lb
 
-        codes = {0: quantize(0, copies(transposes(0)))}
+        def finish_first(h, lb):
+            rows = GROUPS[0][1]
+            for r in range(rows):
+                if h == 0 and r == 0:
+                    plain_cast(False, o8_of[(h, 0)][:, r * L + P:(r + 1) * L], res_of[(h, 0)][:, 0:L - P])
+                scaled_cast(r == 1, o8_of[(h, 0)][:, r * L:r * L + P], lb[:, r, :], fac[(h, 0)][:, r:r + 1])
+            nc.sync.dma_start(
+                out=out_1[:, h, 0:P, :].rearrange("b (a r) j -> a b (r j)", r=rows), in_=o8_of[(h, 0)][:].bitcast(U8),
+            )
+
+        for h in range(H):
+            for j in range(n_groups):
+                if h == 0 or j in OWN_TILES:
+                    nc.vector.memset(
+                        res_of[(h, j)][:].rearrange("p (r y) -> p r y", r=GROUPS[j][1])[:, :, 0:RUN - need[j]], 0.0,
+                    )
+
+        for j in range(1, n_groups):
+            last = (GROUPS[j][1] - 1) * RUN
+            if need[j] < L:
+                plain_cast(
+                    True, o8_of[(0, j)][:, -(-last // 4) * 4:(last + RUN - need[j]) // 4 * 4],
+                    res_of[(0, j)][:, -(-last // 4) * 4:(last + RUN - need[j]) // 4 * 4],
+                )
+        plain_cast(True, o8_of[(0, 0)][:, L + P:2 * L], res_of[(0, 0)][:, 0:L - P])
+
+        group_end = {}
+        for k in range(n_units):
+            h, j, r = units[k]
+            if r == GROUPS[j][1] - 1:
+                group_end[k] = (h, j)
+
+        for part in plan[0:AHEAD]:
+            for job in part:
+                quantize(job, copy_out(transposes(job)))
         loaded = {}
-        for s in range(n_steps + 1):
-            nxt = s + 1
-            made = None
+        for k in range(n_units + 1 + CAST_LAG):
+            fresh = plan[k + AHEAD] if k + AHEAD < n_units else []
+            turned = [transposes(job) for job in fresh]
             banks = None
-            if nxt < n_steps:
-                made = transposes(nxt)
-            if s < n_steps:
-                banks = multiply(s, codes[s])
-                empty_diag(s, banks)
-            both = None
-            if nxt < n_steps:
-                both = copies(made)
-            if s < n_steps:
-                empty_rest(s, banks)
-            if nxt < n_steps:
-                codes[nxt] = quantize(nxt, both)
-            if s >= 1 and steps[s - 1][1] > 0:
-                finish(s - 1)
+            if k < n_units:
+                banks = multiply(k)
+                empty_diag(k, banks)
+            grouped = [copy_out(xt) for xt in turned]
+            if k < n_units:
+                empty_rest(k, banks)
+                if k in group_end:
+                    store_rows(group_end[k][0], group_end[k][1])
+            for n in range(len(fresh)):
+                quantize(fresh[n], grouped[n])
+            if 1 <= k <= n_units:
+                row_maximum(k - 1)
+            if k - 1 - CAST_LAG in group_end and group_end[k - 1 - CAST_LAG][1] > 0:
+                finish(group_end[k - 1 - CAST_LAG][0], group_end[k - 1 - CAST_LAG][1])
             for h in range(H):
-                if s == h * NT + BACK_AFTER:
-                    loaded[h] = load_back(h * NT)
-                if s == h * NT + CAST_AFTER[h]:
-                    finish_first(h * NT, loaded[h])
-            if s < n_steps:
-                row_factors(s)
+                first_end = h * (n_units // H) + GROUPS[0][1] - 1
+                if k == first_end + BACK_AFTER:
+                    loaded[h] = load_back(h)
+                if k == first_end + CAST_AFTER[h]:
+                    finish_first(h, loaded[h])

@@ -70,6 +70,8 @@ def tile_subsampledrelativeattention_kernel(tc, q, e, out_0, out_1):
         make_identity(nc, ident[:])
         zcol = keep.tile([P, 1], F32, name="zcol")
         nc.vector.memset(zcol[:], 0.0)
+        zeros = keep.tile([P, L - P], F32, name="zeros")
+        nc.vector.memset(zeros[:], 0.0)
 
         part_i = keep.tile([P, 1], I32, name="part_i")
         nc.gpsimd.iota(part_i[:], pattern=[[0, 1]], base=0, channel_multiplier=1)
@@ -231,7 +233,7 @@ def tile_subsampledrelativeattention_kernel(tc, q, e, out_0, out_1):
             h, j, r = units[k]
             rows = GROUPS[j][1]
             skip = wide[j] - need[j]
-            for c0, bw, acc in banks:
+            for c0, bw, acc in reversed(banks):
                 lo = skip + SLOTS * rows if c0 == 0 else 0
                 d0 = r * RUN + RUN - wide[j] + c0
                 if bw > lo:
@@ -327,21 +329,21 @@ def tile_subsampledrelativeattention_kernel(tc, q, e, out_0, out_1):
                 out=out_1[:, h, 0:P, :].rearrange("b (a r) j -> a b (r j)", r=rows), in_=o8_of[(h, 0)][:].bitcast(U8),
             )
 
-        for h in range(H):
-            for j in range(n_groups):
-                if h == 0 or j in OWN_TILES:
-                    nc.vector.memset(
-                        res_of[(h, j)][:].rearrange("p (r y) -> p r y", r=GROUPS[j][1])[:, :, 0:RUN - need[j]], 0.0,
-                    )
+        def zero_front(h, j):
+            nc.vector.memset(
+                res_of[(h, j)][:].rearrange("p (r y) -> p r y", r=GROUPS[j][1])[:, :, 0:RUN - need[j]], 0.0,
+            )
+
+        zero_front(0, 0)
+        to_zero = [(h, j) for h in range(H) for j in range(1, n_groups) if h == 0 or j in OWN_TILES]
 
         for j in range(1, n_groups):
             last = (GROUPS[j][1] - 1) * RUN
             if need[j] < L:
-                plain_cast(
-                    True, o8_of[(0, j)][:, -(-last // 4) * 4:(last + RUN - need[j]) // 4 * 4],
-                    res_of[(0, j)][:, -(-last // 4) * 4:(last + RUN - need[j]) // 4 * 4],
-                )
-        plain_cast(True, o8_of[(0, 0)][:, L + P:2 * L], res_of[(0, 0)][:, 0:L - P])
+                lo = -(-last // 4) * 4
+                hi = (last + RUN - need[j]) // 4 * 4
+                plain_cast(True, o8_of[(0, j)][:, lo:hi], zeros[:, 0:hi - lo])
+        plain_cast(True, o8_of[(0, 0)][:, L + P:2 * L], zeros[:])
 
         group_end = {}
         for k in range(n_units):
@@ -365,10 +367,12 @@ def tile_subsampledrelativeattention_kernel(tc, q, e, out_0, out_1):
                 empty_rest(k, banks)
                 if k in group_end:
                     store_rows(group_end[k][0], group_end[k][1])
-            for n in range(len(fresh)):
-                quantize(fresh[n], grouped[n])
             if 1 <= k <= n_units:
                 row_maximum(k - 1)
+            if k < len(to_zero):
+                zero_front(to_zero[k][0], to_zero[k][1])
+            for n in range(len(fresh)):
+                quantize(fresh[n], grouped[n])
             if k - 1 - CAST_LAG in group_end and group_end[k - 1 - CAST_LAG][1] > 0:
                 finish(group_end[k - 1 - CAST_LAG][0], group_end[k - 1 - CAST_LAG][1])
             for h in range(H):

@@ -25,6 +25,7 @@ BANK = 512
 GROUPS = ((0, 2), (128, 2), (256, 3), (448, 3), (640, 3), (832, 3))
 ORDER = ((0, 1, 2, 3, 4, 5), (0, 5, 4, 3, 2, 1))
 OWN_TILES = (5,)
+EROWS = 4
 AHEAD = 2
 CAST_LAG = 1
 BACK_AFTER = 4
@@ -45,9 +46,9 @@ def tile_subsampledrelativeattention_kernel(tc, q, e, out_0, out_1):
     have = [NT] * H
     for k in range(n_units):
         h, j, r = units[k]
-        for t in range(have[h] - 1, (L - wide[j]) // P - 1, -1):
+        for t in range(have[h] - 1, (L - wide[j]) // BANK * EROWS - 1, -1):
             wanted.append((k - AHEAD, h, t))
-        have[h] = min(have[h], (L - wide[j]) // P)
+        have[h] = min(have[h], (L - wide[j]) // BANK * EROWS)
     plan = [[] for n in range(n_units)]
     at = n_units
     for due, h, t in reversed(wanted):
@@ -59,7 +60,8 @@ def tile_subsampledrelativeattention_kernel(tc, q, e, out_0, out_1):
 
     with ExitStack() as ctx:
         keep = ctx.enter_context(tc.tile_pool(name="keep", bufs=1))
-        grp = ctx.enter_context(tc.tile_pool(name="grp", bufs=4))
+        grp = ctx.enter_context(tc.tile_pool(name="grp", bufs=3))
+        big = ctx.enter_context(tc.tile_pool(name="big", bufs=2))
         qcp = ctx.enter_context(tc.tile_pool(name="qcp", bufs=4))
         small = ctx.enter_context(tc.tile_pool(name="small", bufs=3))
         back = ctx.enter_context(tc.tile_pool(name="back", bufs=2))
@@ -70,8 +72,6 @@ def tile_subsampledrelativeattention_kernel(tc, q, e, out_0, out_1):
         make_identity(nc, ident[:])
         zcol = keep.tile([P, 1], F32, name="zcol")
         nc.vector.memset(zcol[:], 0.0)
-        zeros = keep.tile([P, L - P], F32, name="zeros")
-        nc.vector.memset(zeros[:], 0.0)
 
         part_i = keep.tile([P, 1], I32, name="part_i")
         nc.gpsimd.iota(part_i[:], pattern=[[0, 1]], base=0, channel_multiplier=1)
@@ -103,12 +103,13 @@ def tile_subsampledrelativeattention_kernel(tc, q, e, out_0, out_1):
         raw_q = {}
         raw_e = {}
         for kind, a0, a1 in jobs:
-            if kind == "e" and a1 % 2 == 1:
-                x = keep.tile([P, 2, D], BF16, name="re%d_%d" % (a0, a1 // 2))
+            if kind == "e" and a1 % EROWS == EROWS - 1:
+                x = keep.tile([P, EROWS, D], BF16, name="re%d_%d" % (a0, a1 // EROWS))
                 nc.sync.dma_start(
-                    out=x[:], in_=e[a0, (a1 - 1) * P:(a1 + 1) * P, :].rearrange("(t p) k -> p t k", p=P),
+                    out=x[:].rearrange("p t k -> p (t k)"),
+                    in_=e[a0, (a1 // EROWS) * BANK:(a1 // EROWS + 1) * BANK, :].rearrange("(p t) k -> p (t k)", t=EROWS),
                 )
-                raw_e[(a0, a1 // 2)] = x
+                raw_e[(a0, a1 // EROWS)] = x
             if kind == "q" and units[a0][2] == 0:
                 h, j, r = units[a0]
                 row0, rows = GROUPS[j]
@@ -160,19 +161,33 @@ def tile_subsampledrelativeattention_kernel(tc, q, e, out_0, out_1):
 
         def transposes(job):
             kind, a0, a1 = job
+            xt = tp.tile([P, 2, 2, P], F32, name="xt", tag="xt")
             if kind == "e":
-                src = raw_e[(a0, a1 // 2)][:, a1 % 2, :]
+                g, half = a1 % EROWS // 2, a1 % 2
+                for t2 in range(2):
+                    words = raw_e[(a0, a1 // EROWS)][:, 2 * half + t2, :].bitcast(F32)
+                    for u in range(2):
+                        nc.tensor.transpose(xt[:, t2, u, :], words[:, 256 * g + u:256 * (g + 1):2], ident[:])
             else:
                 h, j, r = units[a0]
-                src = raw_q[(h, j)][:, r, :]
-            words = src.bitcast(F32)
-            xt = tp.tile([P, 2, 2, P], F32, name="xt", tag="xt")
-            for g in range(2):
-                for u in range(2):
-                    nc.tensor.transpose(xt[:, g, u, :], words[:, 256 * g + u:256 * (g + 1):2], ident[:])
+                words = raw_q[(h, j)][:, r, :].bitcast(F32)
+                for g in range(2):
+                    for u in range(2):
+                        nc.tensor.transpose(xt[:, g, u, :], words[:, 256 * g + u:256 * (g + 1):2], ident[:])
             return xt
 
-        def copy_out(xt):
+        open_e = {}
+
+        def copy_out(job, xt):
+            kind, a0, a1 = job
+            if kind == "e":
+                half = a1 % 2
+                if half == 1:
+                    ge = big.tile([P, P, 2, 2, 4], BF16, name="ge", tag="ge", align_bytes=64)
+                    open_e[a0] = ge
+                ge = open_e[a0]
+                nc.scalar.copy(out=ge[:].bitcast(F32)[:, :, half, :, :], in_=xt[:].rearrange("q t u p -> q p t u"))
+                return ge
             gx = grp.tile([P, 2, P, 4], BF16, name="gx", tag="gx", align_bytes=64)
             nc.scalar.copy(out=gx[:].bitcast(F32), in_=xt[:].rearrange("p g u r -> p g r u"))
             return gx
@@ -182,11 +197,12 @@ def tile_subsampledrelativeattention_kernel(tc, q, e, out_0, out_1):
         def quantize(job, gx):
             kind, a0, a1 = job
             if kind == "e":
-                cols = slice(a1 * P, (a1 + 1) * P)
-                for g in range(2):
+                if a1 % 2 == 0:
+                    g = a1 % EROWS // 2
+                    cols = slice(a1 // EROWS * BANK, (a1 // EROWS + 1) * BANK)
                     nc.vector.quantize_mx(
                         out=ec[a0][:, g, cols].bitcast(FP8X4), scales=es[a0][:, g, cols],
-                        in_=gx[:, g, :, :].rearrange("p r t -> p (r t)"),
+                        in_=gx[:].rearrange("q p a b c -> q (p a b c)"),
                     )
             else:
                 qc = qcp.tile([P, 2 * P], U32, name="qc", tag="qc", align_bytes=64)
@@ -342,8 +358,8 @@ def tile_subsampledrelativeattention_kernel(tc, q, e, out_0, out_1):
             if need[j] < L:
                 lo = -(-last // 4) * 4
                 hi = (last + RUN - need[j]) // 4 * 4
-                plain_cast(True, o8_of[(0, j)][:, lo:hi], zeros[:, 0:hi - lo])
-        plain_cast(True, o8_of[(0, 0)][:, L + P:2 * L], zeros[:])
+                plain_cast(True, o8_of[(0, j)][:, lo:hi], res_of[(0, 0)][:, 0:hi - lo])
+        plain_cast(True, o8_of[(0, 0)][:, L + P:2 * L], res_of[(0, 0)][:, 0:L - P])
 
         group_end = {}
         for k in range(n_units):
@@ -353,7 +369,7 @@ def tile_subsampledrelativeattention_kernel(tc, q, e, out_0, out_1):
 
         for part in plan[0:AHEAD]:
             for job in part:
-                quantize(job, copy_out(transposes(job)))
+                quantize(job, copy_out(job, transposes(job)))
         loaded = {}
         for k in range(n_units + 1 + CAST_LAG):
             fresh = plan[k + AHEAD] if k + AHEAD < n_units else []
@@ -362,7 +378,7 @@ def tile_subsampledrelativeattention_kernel(tc, q, e, out_0, out_1):
             if k < n_units:
                 banks = multiply(k)
                 empty_diag(k, banks)
-            grouped = [copy_out(xt) for xt in turned]
+            grouped = [copy_out(fresh[n], turned[n]) for n in range(len(fresh))]
             if k < n_units:
                 empty_rest(k, banks)
                 if k in group_end:

@@ -26,6 +26,7 @@ GROUPS = ((0, 2), (128, 2), (256, 3), (448, 3), (640, 3), (832, 3))
 ORDER = ((0, 1, 2, 3, 4, 5), (0, 5, 4, 3, 2, 1))
 OWN_TILES = (5,)
 EROWS = 4
+HELD = (1, 2)
 AHEAD = 2
 CAST_LAG = 1
 BACK_AFTER = 4
@@ -255,9 +256,9 @@ def tile_subsampledrelativeattention_kernel(tc, q, e, out_0, out_1):
                 if bw > lo:
                     nc.scalar.copy(out=res_of[(h, j)][:, d0 + lo:d0 + bw], in_=acc[:, lo:bw])
 
-        def store_rows(h, j):
+        def store_rows(h, j, batches):
             row0, rows = GROUPS[j]
-            for b in range(B):
+            for b in batches:
                 if j > 0:
                     lo = row0 * RUN - L
                     nc.sync.dma_start(
@@ -381,8 +382,6 @@ def tile_subsampledrelativeattention_kernel(tc, q, e, out_0, out_1):
             grouped = [copy_out(fresh[n], turned[n]) for n in range(len(fresh))]
             if k < n_units:
                 empty_rest(k, banks)
-                if k in group_end:
-                    store_rows(group_end[k][0], group_end[k][1])
             if 1 <= k <= n_units:
                 row_maximum(k - 1)
             if k < len(to_zero):
@@ -390,7 +389,12 @@ def tile_subsampledrelativeattention_kernel(tc, q, e, out_0, out_1):
             for n in range(len(fresh)):
                 quantize(fresh[n], grouped[n])
             if k - 1 - CAST_LAG in group_end and group_end[k - 1 - CAST_LAG][1] > 0:
-                finish(group_end[k - 1 - CAST_LAG][0], group_end[k - 1 - CAST_LAG][1])
+                done = group_end[k - 1 - CAST_LAG]
+                if done == HELD:
+                    store_rows(done[0], done[1], (1,))
+                finish(done[0], done[1])
+            if k in group_end:
+                store_rows(group_end[k][0], group_end[k][1], (0,) if group_end[k] == HELD else (0, 1))
             for h in range(H):
                 first_end = h * (n_units // H) + GROUPS[0][1] - 1
                 if k == first_end + BACK_AFTER:

from contextlib import ExitStack

import concourse.mybir as mybir
from concourse.masks import make_identity

B, H, L, D = 2, 2, 1024, 1024
FLOPS = B * H * L * (L + 1) * D

F32 = mybir.dt.float32
BF16 = mybir.dt.bfloat16
I32 = mybir.dt.int32
U32 = mybir.dt.uint32
U8 = mybir.dt.uint8
FP8 = mybir.dt.float8_e4m3fn
FP8X4 = mybir.dt.float8_e4m3fn_x4
ALU = mybir.AluOpType
ACT = mybir.ActivationFunctionType
AX = mybir.AxisListType

P = 128
NT = L // P
SLOTS = P // B
RUN = L + 1
BANK = 512
GROUPS = ((0, 2), (128, 2), (256, 3), (448, 3), (640, 3), (832, 3))
ORDER = ((0, 1, 2, 3, 4, 5), (0, 5, 4, 3, 2, 1))
OWN_TILES = (5,)
EROWS = 4
HELD = (1, 2)
AHEAD = 2
CAST_LAG = 1
BACK_AFTER = 4
CAST_AFTER = (16, 12)


def tile_subsampledrelativeattention_kernel(tc, q, e, out_0, out_1):
    nc = tc.nc
    mat0 = out_0.rearrange("b h i j -> b h (i j)")
    mat1 = out_1.rearrange("b h i j -> b h (i j)")
    n_groups = len(GROUPS)
    units = [(h, j, r) for h in range(H) for j in ORDER[h] for r in range(GROUPS[j][1])]
    n_units = len(units)
    need = [row0 + SLOTS * rows for row0, rows in GROUPS]
    wide = [-(-n // P) * P for n in need]

    wanted = []
    have = [NT] * H
    for k in range(n_units):
        h, j, r = units[k]
        for t in range(have[h] - 1, (L - wide[j]) // BANK * EROWS - 1, -1):
            wanted.append((k - AHEAD, h, t))
        have[h] = min(have[h], (L - wide[j]) // BANK * EROWS)
    plan = [[] for n in range(n_units)]
    at = n_units
    for due, h, t in reversed(wanted):
        at = max(min(due, at - 1), -AHEAD)
        plan[AHEAD + at].insert(0, ("e", h, t))
    for k in range(n_units):
        plan[k].append(("q", k, 0))
    jobs = [job for part in plan for job in part]

    with ExitStack() as ctx:
        keep = ctx.enter_context(tc.tile_pool(name="keep", bufs=1))
        grp = ctx.enter_context(tc.tile_pool(name="grp", bufs=3))
        big = ctx.enter_context(tc.tile_pool(name="big", bufs=2))
        qcp = ctx.enter_context(tc.tile_pool(name="qcp", bufs=4))
        small = ctx.enter_context(tc.tile_pool(name="small", bufs=3))
        back = ctx.enter_context(tc.tile_pool(name="back", bufs=2))
        tp = ctx.enter_context(tc.psum_pool(name="tp", bufs=4))
        mm = ctx.enter_context(tc.psum_pool(name="mm", bufs=4))

        ident = keep.tile([P, P], F32, name="ident")
        make_identity(nc, ident[:])
        zcol = keep.tile([P, 1], F32, name="zcol")
        nc.vector.memset(zcol[:], 0.0)

        part_i = keep.tile([P, 1], I32, name="part_i")
        nc.gpsimd.iota(part_i[:], pattern=[[0, 1]], base=0, channel_multiplier=1)
        col_i = keep.tile([P, SLOTS * 3], I32, name="col_i")
        nc.gpsimd.iota(col_i[:], pattern=[[1, SLOTS * 3]], base=0, channel_multiplier=0)
        slot_i = keep.tile([P, 1], I32, name="slot_i")
        nc.vector.tensor_scalar(out=slot_i[:], in0=part_i[:], scalar1=1, scalar2=None, op0=ALU.arith_shift_right)
        slot_f = keep.tile([P, 1], F32, name="slot_f")
        nc.vector.tensor_copy(out=slot_f[:], in_=slot_i[:])
        col_f = keep.tile([P, SLOTS * 3], F32, name="col_f")
        nc.vector.tensor_copy(out=col_f[:], in_=col_i[:])
        mask = {}
        for rows in (2, 3):
            first = keep.tile([P, rows], F32, name="first%d" % rows)
            x = keep.tile([P, rows, SLOTS * rows], F32, name="mask%d" % rows)
            for r in range(rows):
                nc.vector.tensor_scalar(
                    out=first[:, r:r + 1], in0=slot_f[:], scalar1=-1.0 * rows, scalar2=1.0 * (SLOTS * rows - 1 - r),
                    op0=ALU.mult, op1=ALU.add,
                )
                nc.vector.tensor_scalar(
                    out=x[:, r, :], in0=col_f[:, 0:SLOTS * rows], scalar1=first[:, r:r + 1], scalar2=None,
                    op0=ALU.is_ge,
                )
            mask[rows] = x

        ctx.enter_context(tc.manual_schedule())

        raw_q = {}
        raw_e = {}
        for kind, a0, a1 in jobs:
            if kind == "e" and a1 % EROWS == EROWS - 1:
                x = keep.tile([P, EROWS, D], BF16, name="re%d_%d" % (a0, a1 // EROWS))
                nc.sync.dma_start(
                    out=x[:].rearrange("p t k -> p (t k)"),
                    in_=e[a0, (a1 // EROWS) * BANK:(a1 // EROWS + 1) * BANK, :].rearrange("(p t) k -> p (t k)", t=EROWS),
                )
                raw_e[(a0, a1 // EROWS)] = x
            if kind == "q" and units[a0][2] == 0:
                h, j, r = units[a0]
                row0, rows = GROUPS[j]
                x = keep.tile([P, rows, D], BF16, name="rq%d_%d" % (h, j))
                nc.sync.dma_start(
                    out=x[:].rearrange("p r k -> p (r k)"),
                    in_=q[:, h, row0:row0 + SLOTS * rows, :].rearrange("b (a r) k -> a b (r k)", r=rows),
                )
                raw_q[(h, j)] = x

        ec = []
        es = []
        for h in range(H):
            x = keep.tile([P, 2, L], U32, name="ec%d" % h, align_bytes=64)
            ec.append(x)
            x = keep.tile([P, 2, L], U8, name="es%d" % h, align_bytes=64)
            es.append(x)

        res_of = {}
        o8_of = {}
        for h in range(H):
            for j in range(n_groups):
                rows = GROUPS[j][1]
                if h == 0 or j in OWN_TILES:
                    x = keep.tile([P, rows * RUN], F32, name="res%d_%d" % (h, j))
                    res_of[(h, j)] = x
                    x = keep.tile([P, rows * (RUN if j > 0 else L)], FP8, name="o8_%d_%d" % (h, j))
                    o8_of[(h, j)] = x
                else:
                    res_of[(h, j)] = res_of[(0, j)]
                    o8_of[(h, j)] = o8_of[(0, j)]
        fac = {}
        for h in range(H):
            for j in range(n_groups):
                x = keep.tile([P, GROUPS[j][1]], F32, name="fac%d_%d" % (h, j))
                fac[(h, j)] = x

        def plain_cast(on_scalar, out, in_):
            if on_scalar:
                nc.scalar.copy(out=out, in_=in_, saturate=False)
            else:
                nc.vector.tensor_copy(out=out, in_=in_, saturate=False)

        def scaled_cast(on_scalar, out, in_, f):
            if on_scalar:
                nc.scalar.activation(out=out, in_=in_, func=ACT.Identity, scale=f, bias=zcol[:, 0:1], saturate=False)
            else:
                nc.vector.tensor_scalar(out=out, in0=in_, scalar1=f, scalar2=None, op0=ALU.mult, saturate=False)

        def transposes(job):
            kind, a0, a1 = job
            xt = tp.tile([P, 2, 2, P], F32, name="xt", tag="xt")
            if kind == "e":
                g, half = a1 % EROWS // 2, a1 % 2
                for t2 in range(2):
                    words = raw_e[(a0, a1 // EROWS)][:, 2 * half + t2, :].bitcast(F32)
                    for u in range(2):
                        nc.tensor.transpose(xt[:, t2, u, :], words[:, 256 * g + u:256 * (g + 1):2], ident[:])
            else:
                h, j, r = units[a0]
                words = raw_q[(h, j)][:, r, :].bitcast(F32)
                for g in range(2):
                    for u in range(2):
                        nc.tensor.transpose(xt[:, g, u, :], words[:, 256 * g + u:256 * (g + 1):2], ident[:])
            return xt

        open_e = {}

        def copy_out(job, xt):
            kind, a0, a1 = job
            if kind == "e":
                half = a1 % 2
                if half == 1:
                    ge = big.tile([P, P, 2, 2, 4], BF16, name="ge", tag="ge", align_bytes=64)
                    open_e[a0] = ge
                ge = open_e[a0]
                nc.scalar.copy(out=ge[:].bitcast(F32)[:, :, half, :, :], in_=xt[:].rearrange("q t u p -> q p t u"))
                return ge
            gx = grp.tile([P, 2, P, 4], BF16, name="gx", tag="gx", align_bytes=64)
            nc.scalar.copy(out=gx[:].bitcast(F32), in_=xt[:].rearrange("p g u r -> p g r u"))
            return gx

        codes = {}

        def quantize(job, gx):
            kind, a0, a1 = job
            if kind == "e":
                if a1 % 2 == 0:
                    g = a1 % EROWS // 2
                    cols = slice(a1 // EROWS * BANK, (a1 // EROWS + 1) * BANK)
                    nc.vector.quantize_mx(
                        out=ec[a0][:, g, cols].bitcast(FP8X4), scales=es[a0][:, g, cols],
                        in_=gx[:].rearrange("q p a b c -> q (p a b c)"),
                    )
            else:
                qc = qcp.tile([P, 2 * P], U32, name="qc", tag="qc", align_bytes=64)
                qs = qcp.tile([P, 2 * P], U8, name="qs", tag="qs", align_bytes=64)
                nc.vector.quantize_mx(
                    out=qc[:].bitcast(FP8X4), scales=qs[:], in_=gx[:].rearrange("p g r t -> p (g r t)"),
                )
                codes[a0] = (qc, qs)

        def multiply(k):
            h, j, r = units[k]
            m0 = L - wide[j]
            qc, qs = codes[k]
            banks = []
            for c0 in range(0, wide[j], BANK):
                bw = min(BANK, wide[j] - c0)
                acc = mm.tile([P, BANK], F32, name="acc", tag="acc")
                pieces = [(0, 256), (256, 128)] if bw == 384 else [(0, bw)]
                for g0, n in pieces:
                    cols = slice(m0 + c0 + g0, m0 + c0 + g0 + n)
                    for g in range(2):
                        w = slice(g * P, (g + 1) * P)
                        nc.tensor.matmul_mx(
                            out=acc[:, g0:g0 + n],
                            lhsT=qc[:, w].bitcast(FP8X4), lhsT_scale=qs[:, w],
                            rhs=ec[h][:, g, cols].bitcast(FP8X4), rhs_scale=es[h][:, g, cols],
                            start=(g == 0), stop=(g == 1),
                        )
                banks.append((c0, bw, acc))
            return banks

        def empty_diag(k, banks):
            h, j, r = units[k]
            rows = GROUPS[j][1]
            skip = wide[j] - need[j]
            d0 = r * RUN + RUN - wide[j] + skip
            c0, bw, acc = banks[0]
            nc.vector.tensor_tensor(
                out=res_of[(h, j)][:, d0:d0 + SLOTS * rows], in0=acc[:, skip:skip + SLOTS * rows], in1=mask[rows][:, r, :],
                op=ALU.mult,
            )

        def empty_rest(k, banks):
            h, j, r = units[k]
            rows = GROUPS[j][1]
            skip = wide[j] - need[j]
            for c0, bw, acc in reversed(banks):
                lo = skip + SLOTS * rows if c0 == 0 else 0
                d0 = r * RUN + RUN - wide[j] + c0
                if bw > lo:
                    nc.scalar.copy(out=res_of[(h, j)][:, d0 + lo:d0 + bw], in_=acc[:, lo:bw])

        def store_rows(h, j, batches):
            row0, rows = GROUPS[j]
            for b in batches:
                if j > 0:
                    lo = row0 * RUN - L
                    nc.sync.dma_start(
                        out=mat0[b, h, lo:lo + SLOTS * rows * RUN].rearrange("(a y) -> a y", y=rows * RUN),
                        in_=res_of[(h, j)][b:P:B, :],
                    )
                else:
                    nc.sync.dma_start(
                        out=mat0[b, h, 0:SLOTS * rows * RUN].rearrange("(a y) -> a y", y=rows * RUN)[:, 0:RUN + 1],
                        in_=res_of[(h, 0)][b:P:B, L:rows * RUN],
                    )
                    nc.gpsimd.dma_start(
                        out=mat0[b, h, RUN + 1:RUN + 1 + (SLOTS - 1) * rows * RUN].rearrange(
                            "(a y) -> a y", y=rows * RUN)[:, 0:L],
                        in_=res_of[(h, 0)][B + b:P:B, 0:L],
                    )

        maxima = {}

        def row_maximum(k):
            h, j, r = units[k]
            rows = GROUPS[j][1]
            if r == 0:
                am = small.tile([P, rows], F32, name="am", tag="am")
                maxima[(h, j)] = am
            am = maxima[(h, j)]
            nc.vector.tensor_reduce(
                out=am[:, r:r + 1], in_=res_of[(h, j)][:, r * RUN + RUN - need[j]:(r + 1) * RUN], axis=AX.X, op=ALU.max,
                apply_absolute_value=True,
            )
            if r == rows - 1:
                rc = small.tile([P, rows], F32, name="rc", tag="rc")
                nc.vector.reciprocal(out=rc[:], in_=am[:])
                nc.gpsimd.tensor_scalar(
                    out=fac[(h, j)][:], in0=rc[:], scalar1=448.0, scalar2=0.0, op0=ALU.mult, op1=ALU.add,
                )

        def finish(h, j):
            row0, rows = GROUPS[j]
            z = RUN - need[j]
            f = fac[(h, j)]
            new = h == 0 or j in OWN_TILES
            last = (rows - 1) * RUN
            if h == 0 or rows == 2:
                cut = -(-last // 4) * 4 if z == 1 else (last + z) // 4 * 4
            else:
                cut = (last - need[j] // 2) // 4 * 4
            for r in range(rows):
                lo = r * RUN + (0 if new else z)
                hi = (r + 1) * RUN
                if h == 0 and z > 1 and r == rows - 1:
                    lo = cut
                if h == 0 and z > 1 and r == rows - 2:
                    hi = -(-last // 4) * 4
                if lo < cut:
                    scaled_cast(
                        False, o8_of[(h, j)][:, lo:min(hi, cut)], res_of[(h, j)][:, lo:min(hi, cut)], f[:, r:r + 1],
                    )
                if hi > cut:
                    scaled_cast(
                        True, o8_of[(h, j)][:, max(lo, cut):hi], res_of[(h, j)][:, max(lo, cut):hi], f[:, r:r + 1],
                    )
            lo = row0 * RUN - L
            nc.sync.dma_start(
                out=mat1[:, h, lo:lo + SLOTS * rows * RUN].rearrange("b (a y) -> a b y", y=rows * RUN),
                in_=o8_of[(h, j)][:].bitcast(U8),
            )

        def load_back(h):
            rows = GROUPS[0][1]
            lb = back.tile([P, rows, P], F32, name="lb", tag="lb")
            for b in range(B):
                nc.sync.dma_start(
                    out=lb[b:P:B, :, :], in_=out_0[b, h, 0:P, 0:P].rearrange("(a r) j -> a r j", r=rows),
                )
            return lb

        def finish_first(h, lb):
            rows = GROUPS[0][1]
            for r in range(rows):
                if h == 0 and r == 0:
                    plain_cast(False, o8_of[(h, 0)][:, r * L + P:(r + 1) * L], res_of[(h, 0)][:, 0:L - P])
                scaled_cast(r == 1, o8_of[(h, 0)][:, r * L:r * L + P], lb[:, r, :], fac[(h, 0)][:, r:r + 1])
            nc.sync.dma_start(
                out=out_1[:, h, 0:P, :].rearrange("b (a r) j -> a b (r j)", r=rows), in_=o8_of[(h, 0)][:].bitcast(U8),
            )

        def zero_front(h, j):
            nc.vector.memset(
                res_of[(h, j)][:].rearrange("p (r y) -> p r y", r=GROUPS[j][1])[:, :, 0:RUN - need[j]], 0.0,
            )

        zero_front(0, 0)
        to_zero = [(h, j) for h in range(H) for j in range(1, n_groups) if h == 0 or j in OWN_TILES]

        for j in range(1, n_groups):
            last = (GROUPS[j][1] - 1) * RUN
            if need[j] < L:
                lo = -(-last // 4) * 4
                hi = (last + RUN - need[j]) // 4 * 4
                plain_cast(True, o8_of[(0, j)][:, lo:hi], res_of[(0, 0)][:, 0:hi - lo])
        plain_cast(True, o8_of[(0, 0)][:, L + P:2 * L], res_of[(0, 0)][:, 0:L - P])

        group_end = {}
        for k in range(n_units):
            h, j, r = units[k]
            if r == GROUPS[j][1] - 1:
                group_end[k] = (h, j)

        for part in plan[0:AHEAD]:
            for job in part:
                quantize(job, copy_out(job, transposes(job)))
        loaded = {}
        for k in range(n_units + 1 + CAST_LAG):
            fresh = plan[k + AHEAD] if k + AHEAD < n_units else []
            turned = [transposes(job) for job in fresh]
            banks = None
            if k < n_units:
                banks = multiply(k)
                empty_diag(k, banks)
            grouped = [copy_out(fresh[n], turned[n]) for n in range(len(fresh))]
            if k < n_units:
                empty_rest(k, banks)
            if 1 <= k <= n_units:
                row_maximum(k - 1)
            if k < len(to_zero):
                zero_front(to_zero[k][0], to_zero[k][1])
            for n in range(len(fresh)):
                quantize(fresh[n], grouped[n])
            if k - 1 - CAST_LAG in group_end and group_end[k - 1 - CAST_LAG][1] > 0:
                done = group_end[k - 1 - CAST_LAG]
                if done == HELD:
                    store_rows(done[0], done[1], (1,))
                finish(done[0], done[1])
            if k in group_end:
                store_rows(group_end[k][0], group_end[k][1], (0,) if group_end[k] == HELD else (0, 1))
            for h in range(H):
                first_end = h * (n_units // H) + GROUPS[0][1] - 1
                if k == first_end + BACK_AFTER:
                    loaded[h] = load_back(h)
                if k == first_end + CAST_AFTER[h]:
                    finish_first(h, loaded[h])
